import numpy as np
import ml_dtypes


def mxq(x, axis, fmt="e4m3"):
    dtype, down = {"e4m3": (ml_dtypes.float8_e4m3fn, 7), "e5m2": (ml_dtypes.float8_e5m2, 14)}[fmt]
    v = np.moveaxis(np.asarray(x, np.float32).astype(ml_dtypes.bfloat16).astype(np.float64), axis, -1)
    blocks = v.reshape(v.shape[:-1] + (-1, 32))
    amax = np.abs(blocks).max(-1, keepdims=True)
    byte = np.maximum(np.where(amax > 0, np.frexp(amax)[1] - 1 + 127, 0) - down, 1)
    scale = np.exp2(byte - 127.0)
    codes = (blocks / scale).astype(np.float32).astype(dtype).astype(np.float64)
    return np.moveaxis((codes * scale).reshape(v.shape), -1, axis)


WIDE = False


def mx_kscale(k):
    if not WIDE:
        return np.ones(k)
    levels = np.array([10, -10, 5, -5, 0])
    a = np.random.permutation(np.resize(levels, k // 512 * 4)).reshape(k // 512, 4)
    idx = np.arange(k)
    return np.exp2(a[idx // 512, idx % 128 // 32])


BF16 = ml_dtypes.bfloat16


def bf(x):
    return np.asarray(x, np.float32).astype(BF16)


def f64(x):
    return np.asarray(x).astype(np.float64)


B, C, H, W = 1, 2048, 32, 64
CK, CV = C // 8, C // 2
HP, WP = H // 2, W // 2
N, M = H * W, HP * WP


def maxpool2x2(v):
    return v.reshape(v.shape[0], v.shape[1], HP, 2, WP, 2).max(axis=(3, 5))


def setup_inputs():
    s = mx_kscale(C)
    a = 1.7 / CK ** 0.25
    return {"x": bf(np.random.standard_normal((B, C, H, W)) * s[:, None, None]),
            "w_phi": bf(np.random.standard_normal((CK, C)) * a / np.sqrt(C) / s),
            "w_g": bf(np.random.standard_normal((CV, C)) / np.sqrt(C) / s)}


def reference(x, w_phi, w_g):
    xq = mxq(f64(x).reshape(B, C, N), 1, "e4m3")
    u_phi = (mxq(f64(w_phi), 1, "e4m3") @ xq).reshape(B, CK, H, W)
    u_g = (mxq(f64(w_g), 1, "e4m3") @ xq).reshape(B, CV, H, W)
    phi = maxpool2x2(u_phi).reshape(B, CK, M)
    g = maxpool2x2(u_g).reshape(B, CV, M)
    return phi, g

@@ -1,0 +1,203 @@
+from contextlib import ExitStack
+
+import concourse.mybir as mybir
+from concourse.masks import make_identity
+
+BF16 = mybir.dt.bfloat16
+F32 = mybir.dt.float32
+U32 = mybir.dt.uint32
+U8 = mybir.dt.uint8
+FP8X4 = mybir.dt.float8_e4m3fn_x4
+
+P = 128
+PACK = 4
+K_PASS = P * PACK
+C = 2048
+PASSES = C // K_PASS
+HEIGHT, WIDTH = 32, 64
+PIXELS = HEIGHT * WIDTH
+N_BLOCK = 512
+N_BLOCKS = PIXELS // N_BLOCK
+POOLED_ROWS = N_BLOCK // WIDTH // 2
+POOLED_WIDTH = WIDTH // 2
+POOLED_BLOCK = POOLED_ROWS * POOLED_WIDTH
+PHI_TILES = 256 // P
+G_TILES = 1024 // P
+M_TILES = PHI_TILES + G_TILES
+WORDS = P
+WORD_BLOCKS = C // 2 // WORDS
+BANK_BLOCKS = 4
+FIRST_TILES = 4
+WEIGHTS_AHEAD = 2
+
+FLOPS = 2 * (PHI_TILES + G_TILES) * P * C * PIXELS
+
+
+def tile_attention_pa_kernel(tc, x, w_phi, w_g, out_0, out_1):
+    nc = tc.nc
+    x_rows = x.rearrange("b c h w -> (b c) (h w)")
+    phi_rows = out_0.rearrange("b o m -> (b o) m")
+    g_rows = out_1.rearrange("b o m -> (b o) m")
+
+    def weight_rows(m):
+        if m < PHI_TILES:
+            return w_phi[m * P : (m + 1) * P, :]
+        return w_g[(m - PHI_TILES) * P : (m - PHI_TILES + 1) * P, :]
+
+    def output_rows(m):
+        if m < PHI_TILES:
+            return phi_rows[m * P : (m + 1) * P, :]
+        return g_rows[(m - PHI_TILES) * P : (m - PHI_TILES + 1) * P, :]
+
+    with ExitStack() as ctx:
+        keep = ctx.enter_context(tc.tile_pool(name="keep", bufs=1))
+        w_stage = ctx.enter_context(tc.tile_pool(name="w_stage", bufs=2))
+        x_stage = ctx.enter_context(tc.tile_pool(name="x_stage", bufs=3))
+        sums = ctx.enter_context(tc.psum_pool(name="sums", bufs=4))
+        turned = ctx.enter_context(tc.psum_pool(name="turned", bufs=4))
+
+        identity = keep.tile([P, P], F32, name="identity")
+        make_identity(nc, identity[:])
+
+        w_raw = [keep.tile([P, C], BF16, name="w_raw%d" % m) for m in range(M_TILES)]
+        w_codes = [
+            keep.tile([P, PASSES * P], U32, name="w_codes%d" % m, align_bytes=64)
+            for m in range(M_TILES)
+        ]
+        w_scales = [
+            keep.tile([P, PASSES * P], U8, name="w_scales%d" % m, align_bytes=64)
+            for m in range(M_TILES)
+        ]
+        x_raw = [
+            [keep.tile([P, PACK, N_BLOCK], BF16, name="x_raw%d_%d" % (b, g)) for g in range(PASSES)]
+            for b in range(N_BLOCKS)
+        ]
+        x_codes = [
+            [
+                keep.tile([P, N_BLOCK], U32, name="x_codes%d_%d" % (b, g), align_bytes=64)
+                for g in range(PASSES)
+            ]
+            for b in range(N_BLOCKS)
+        ]
+        x_scales = [
+            [
+                keep.tile([P, N_BLOCK], U8, name="x_scales%d_%d" % (b, g), align_bytes=64)
+                for g in range(PASSES)
+            ]
+            for b in range(N_BLOCKS)
+        ]
+
+        def load_weights(m):
+            nc.sync.dma_start(out=w_raw[m][:], in_=weight_rows(m))
+
+        def load_x(b, g):
+            for u in range(2):
+                first = g * K_PASS + u * 2 * P
+                nc.sync.dma_start(
+                    out=x_raw[b][g][:, 2 * u : 2 * u + 2, :],
+                    in_=x_rows[
+                        first : first + 2 * P, b * N_BLOCK : (b + 1) * N_BLOCK
+                    ].rearrange("(p e) n -> p e n", e=2),
+                )
+
+        def prepare_weights(m):
+            grouped = w_stage.tile([P, C], BF16, name="w_grouped", tag="w_grouped", align_bytes=64)
+            grouped_words = grouped[:].bitcast(F32).rearrange(
+                "p (g o u) -> p g o u", g=PASSES, o=P, u=2
+            )
+            raw_words = w_raw[m][:].bitcast(F32)
+            passes_in_bank = BANK_BLOCKS // 2
+            for bank in range(WORD_BLOCKS // BANK_BLOCKS):
+                flipped = turned.tile([P, BANK_BLOCKS, P], F32, name="flipped", tag="flipped")
+                for q in range(BANK_BLOCKS):
+                    j = bank * BANK_BLOCKS + q
+                    nc.tensor.transpose(
+                        flipped[:, q, :], raw_words[:, j * WORDS : (j + 1) * WORDS], identity[:]
+                    )
+                nc.scalar.copy(
+                    out=grouped_words[:, bank * passes_in_bank : (bank + 1) * passes_in_bank],
+                    in_=flipped[:].rearrange("p (g u) o -> p g o u", u=2),
+                )
+            nc.vector.quantize_mx(
+                out=w_codes[m][:].bitcast(FP8X4), scales=w_scales[m][:], in_=grouped[:]
+            )
+
+        def prepare_x(b, g):
+            grouped = x_stage.tile(
+                [P, N_BLOCK, PACK], BF16, name="x_grouped", tag="x_grouped", align_bytes=64
+            )
+            target = grouped[:].rearrange("p (c r) t -> p c t r", r=4)
+            source = x_raw[b][g][:].rearrange("p t (c r) -> p c t r", r=4)
+            if b == 0:
+                nc.vector.tensor_copy(out=target, in_=source)
+            else:
+                nc.scalar.copy(out=target, in_=source)
+            nc.vector.quantize_mx(
+                out=x_codes[b][g][:].bitcast(FP8X4),
+                scales=x_scales[b][g][:],
+                in_=grouped[:].rearrange("p n t -> p (n t)"),
+            )
+
+        def new_sum():
+            return sums.tile([P, N_BLOCK], F32, name="acc", tag="acc")
+
+        def multiply(acc, b, m, g):
+            nc.tensor.matmul_mx(
+                out=acc[:],
+                lhsT=w_codes[m][:, g * P : (g + 1) * P].bitcast(FP8X4),
+                lhsT_scale=w_scales[m][:, g * P : (g + 1) * P],
+                rhs=x_codes[b][g][:].bitcast(FP8X4),
+                rhs_scale=x_scales[b][g][:],
+                start=(g == 0),
+                stop=(g == PASSES - 1),
+            )
+
+        def pool_and_store(acc, b, m):
+            pooled = keep.tile([P, POOLED_ROWS, POOLED_WIDTH], F32, name="pooled%d_%d" % (b, m))
+            nc.vector.tensor_reduce(
+                out=pooled[:],
+                in_=acc[:].rearrange(
+                    "p (i a j b) -> p i j a b", i=POOLED_ROWS, a=2, j=POOLED_WIDTH, b=2
+                ),
+                axis=mybir.AxisListType.XY,
+                op=mybir.AluOpType.max,
+            )
+            nc.sync.dma_start(
+                out=output_rows(m)[:, b * POOLED_BLOCK : (b + 1) * POOLED_BLOCK],
+                in_=pooled[:].rearrange("p i j -> p (i j)"),
+            )
+
+        for m in range(FIRST_TILES):
+            load_weights(m)
+        for g in range(PASSES):
+            load_x(0, g)
+        for m in range(FIRST_TILES, M_TILES):
+            load_weights(m)
+        for b in range(1, N_BLOCKS):
+            for g in range(PASSES):
+                load_x(b, g)
+
+        for m in range(FIRST_TILES + WEIGHTS_AHEAD):
+            prepare_weights(m)
+        for g in range(PASSES):
+            prepare_x(0, g)
+        first_sums = [new_sum() for m in range(FIRST_TILES)]
+        for g in range(PASSES):
+            for m in range(FIRST_TILES):
+                multiply(first_sums[m], 0, m, g)
+        for m in range(FIRST_TILES):
+            pool_and_store(first_sums[m], 0, m)
+
+        for b in range(N_BLOCKS):
+            first_tile = FIRST_TILES if b == 0 else 0
+            tiles = M_TILES - first_tile
+            for m in range(first_tile, M_TILES):
+                if b == 0 and m + WEIGHTS_AHEAD < M_TILES:
+                    prepare_weights(m + WEIGHTS_AHEAD)
+                for g in range(PASSES):
+                    if b + 1 < N_BLOCKS and g * tiles // PASSES == m - first_tile:
+                        prepare_x(b + 1, g)
+                acc = new_sum()
+                for g in range(PASSES):
+                    multiply(acc, b, m, g)
+                pool_and_store(acc, b, m)

@@ -29,8 +29,14 @@ WORD_BLOCKS = C // 2 // WORDS
 BANK_BLOCKS = 4
 FIRST_TILES = 4
 WEIGHTS_AHEAD = 2
+RUN = 4
+SHARED_BLOCKS = 2
+BLOCK_1_FROM = 5
+POOL_LAG = 2
+SUM_BANKS = 6
+TILES = M_TILES * N_BLOCKS
 
-FLOPS = 2 * (PHI_TILES + G_TILES) * P * C * PIXELS
+FLOPS = 2 * M_TILES * P * C * PIXELS
 
 
 def tile_attention_pa_kernel(tc, x, w_phi, w_g, out_0, out_1):
@@ -51,10 +57,11 @@ def tile_attention_pa_kernel(tc, x, w_phi, w_g, out_0, out_1):
 
     with ExitStack() as ctx:
         keep = ctx.enter_context(tc.tile_pool(name="keep", bufs=1))
-        w_stage = ctx.enter_context(tc.tile_pool(name="w_stage", bufs=2))
+        w_stage = ctx.enter_context(tc.tile_pool(name="w_stage", bufs=3))
         x_stage = ctx.enter_context(tc.tile_pool(name="x_stage", bufs=3))
-        sums = ctx.enter_context(tc.psum_pool(name="sums", bufs=4))
-        turned = ctx.enter_context(tc.psum_pool(name="turned", bufs=4))
+        sums = ctx.enter_context(tc.psum_pool(name="sums", bufs=SUM_BANKS))
+        turned = ctx.enter_context(tc.psum_pool(name="turned", bufs=8 - SUM_BANKS))
+        ctx.enter_context(tc.manual_schedule())
 
         identity = keep.tile([P, P], F32, name="identity")
         make_identity(nc, identity[:])
@@ -86,6 +93,10 @@ def tile_attention_pa_kernel(tc, x, w_phi, w_g, out_0, out_1):
             ]
             for b in range(N_BLOCKS)
         ]
+        w_grouped = {}
+        x_grouped = {}
+        open_sums = {}
+        pooled_tiles = []
 
         def load_weights(m):
             nc.sync.dma_start(out=w_raw[m][:], in_=weight_rows(m))
@@ -100,7 +111,7 @@ def tile_attention_pa_kernel(tc, x, w_phi, w_g, out_0, out_1):
                     ].rearrange("(p e) n -> p e n", e=2),
                 )
 
-        def prepare_weights(m):
+        def flip_weights(m):
             grouped = w_stage.tile([P, C], BF16, name="w_grouped", tag="w_grouped", align_bytes=64)
             grouped_words = grouped[:].bitcast(F32).rearrange(
                 "p (g o u) -> p g o u", g=PASSES, o=P, u=2
@@ -118,32 +129,39 @@ def tile_attention_pa_kernel(tc, x, w_phi, w_g, out_0, out_1):
                     out=grouped_words[:, bank * passes_in_bank : (bank + 1) * passes_in_bank],
                     in_=flipped[:].rearrange("p (g u) o -> p g o u", u=2),
                 )
+            w_grouped[m] = grouped
+
+        def quantise_weights(m):
             nc.vector.quantize_mx(
-                out=w_codes[m][:].bitcast(FP8X4), scales=w_scales[m][:], in_=grouped[:]
+                out=w_codes[m][:].bitcast(FP8X4), scales=w_scales[m][:], in_=w_grouped[m][:]
             )
 
-        def prepare_x(b, g):
+        def regroup_x(b, g):
             grouped = x_stage.tile(
                 [P, N_BLOCK, PACK], BF16, name="x_grouped", tag="x_grouped", align_bytes=64
             )
-            target = grouped[:].rearrange("p (c r) t -> p c t r", r=4)
-            source = x_raw[b][g][:].rearrange("p t (c r) -> p c t r", r=4)
-            if b == 0:
-                nc.vector.tensor_copy(out=target, in_=source)
-            else:
-                nc.scalar.copy(out=target, in_=source)
+            target = grouped[:].rearrange("p (c r) t -> p c t r", r=RUN)
+            source = x_raw[b][g][:].rearrange("p t (c r) -> p c t r", r=RUN)
+            vector_runs = N_BLOCK // RUN // 2 if b < SHARED_BLOCKS else 0
+            if vector_runs > 0:
+                nc.vector.tensor_copy(out=target[:, :vector_runs], in_=source[:, :vector_runs])
+            nc.scalar.copy(out=target[:, vector_runs:], in_=source[:, vector_runs:])
+            x_grouped[(b, g)] = grouped
+
+        def quantise_x(b, g):
             nc.vector.quantize_mx(
                 out=x_codes[b][g][:].bitcast(FP8X4),
                 scales=x_scales[b][g][:],
-                in_=grouped[:].rearrange("p n t -> p (n t)"),
+                in_=x_grouped[(b, g)][:].rearrange("p n t -> p (n t)"),
             )
 
-        def new_sum():
-            return sums.tile([P, N_BLOCK], F32, name="acc", tag="acc")
+        def open_sum(s):
+            open_sums[s] = sums.tile([P, N_BLOCK], F32, name="acc", tag="acc")
 
-        def multiply(acc, b, m, g):
+        def multiply(s, g):
+            b, m = divmod(s, M_TILES)
             nc.tensor.matmul_mx(
-                out=acc[:],
+                out=open_sums[s][:],
                 lhsT=w_codes[m][:, g * P : (g + 1) * P].bitcast(FP8X4),
                 lhsT_scale=w_scales[m][:, g * P : (g + 1) * P],
                 rhs=x_codes[b][g][:].bitcast(FP8X4),
@@ -152,20 +170,23 @@ def tile_attention_pa_kernel(tc, x, w_phi, w_g, out_0, out_1):
                 stop=(g == PASSES - 1),
             )
 
-        def pool_and_store(acc, b, m):
-            pooled = keep.tile([P, POOLED_ROWS, POOLED_WIDTH], F32, name="pooled%d_%d" % (b, m))
-            nc.vector.tensor_reduce(
-                out=pooled[:],
-                in_=acc[:].rearrange(
-                    "p (i a j b) -> p i j a b", i=POOLED_ROWS, a=2, j=POOLED_WIDTH, b=2
-                ),
-                axis=mybir.AxisListType.XY,
-                op=mybir.AluOpType.max,
-            )
-            nc.sync.dma_start(
-                out=output_rows(m)[:, b * POOLED_BLOCK : (b + 1) * POOLED_BLOCK],
-                in_=pooled[:].rearrange("p i j -> p (i j)"),
-            )
+        def pool_tiles_before(limit):
+            for s in range(len(pooled_tiles), limit):
+                b, m = divmod(s, M_TILES)
+                pooled = keep.tile([P, POOLED_ROWS, POOLED_WIDTH], F32, name="pooled%d" % s)
+                nc.vector.tensor_reduce(
+                    out=pooled[:],
+                    in_=open_sums[s][:].rearrange(
+                        "p (i a j b) -> p i j a b", i=POOLED_ROWS, a=2, j=POOLED_WIDTH, b=2
+                    ),
+                    axis=mybir.AxisListType.XY,
+                    op=mybir.AluOpType.max,
+                )
+                nc.sync.dma_start(
+                    out=output_rows(m)[:, b * POOLED_BLOCK : (b + 1) * POOLED_BLOCK],
+                    in_=pooled[:].rearrange("p i j -> p (i j)"),
+                )
+                pooled_tiles.append(s)
 
         for m in range(FIRST_TILES):
             load_weights(m)
@@ -177,27 +198,43 @@ def tile_attention_pa_kernel(tc, x, w_phi, w_g, out_0, out_1):
             for g in range(PASSES):
                 load_x(b, g)
 
-        for m in range(FIRST_TILES + WEIGHTS_AHEAD):
-            prepare_weights(m)
-        for g in range(PASSES):
-            prepare_x(0, g)
-        first_sums = [new_sum() for m in range(FIRST_TILES)]
-        for g in range(PASSES):
-            for m in range(FIRST_TILES):
-                multiply(first_sums[m], 0, m, g)
         for m in range(FIRST_TILES):
-            pool_and_store(first_sums[m], 0, m)
+            flip_weights(m)
+            quantise_weights(m)
+            open_sum(m)
 
-        for b in range(N_BLOCKS):
-            first_tile = FIRST_TILES if b == 0 else 0
-            tiles = M_TILES - first_tile
-            for m in range(first_tile, M_TILES):
-                if b == 0 and m + WEIGHTS_AHEAD < M_TILES:
-                    prepare_weights(m + WEIGHTS_AHEAD)
+        regroup_x(0, 0)
+        for step in range(M_TILES):
+            if step + 1 < PASSES:
+                regroup_x(0, step + 1)
+            if FIRST_TILES <= step + WEIGHTS_AHEAD < M_TILES:
+                flip_weights(step + WEIGHTS_AHEAD)
+            if 0 <= step - BLOCK_1_FROM < PASSES:
+                regroup_x(1, step - BLOCK_1_FROM)
+            if step < PASSES:
+                quantise_x(0, step)
+            if FIRST_TILES <= step + WEIGHTS_AHEAD - 1 < M_TILES:
+                quantise_weights(step + WEIGHTS_AHEAD - 1)
+            if 0 <= step - BLOCK_1_FROM - 1 < PASSES:
+                quantise_x(1, step - BLOCK_1_FROM - 1)
+            if step < PASSES:
+                for m in range(FIRST_TILES):
+                    multiply(m, step)
+            else:
+                pool_tiles_before(step - POOL_LAG)
+                open_sum(step)
                 for g in range(PASSES):
-                    if b + 1 < N_BLOCKS and g * tiles // PASSES == m - first_tile:
-                        prepare_x(b + 1, g)
-                acc = new_sum()
-                for g in range(PASSES):
-                    multiply(acc, b, m, g)
-                pool_and_store(acc, b, m)
+                    multiply(step, g)
+
+        for s in range(M_TILES, TILES):
+            b, m = divmod(s, M_TILES)
+            for g in range(PASSES):
+                if b + 1 < N_BLOCKS and g * M_TILES // PASSES == m:
+                    regroup_x(b + 1, g)
+                if b + 1 < N_BLOCKS and g * M_TILES // PASSES + 2 == m:
+                    quantise_x(b + 1, g)
+            pool_tiles_before(s - POOL_LAG)
+            open_sum(s)
+            for g in range(PASSES):
+                multiply(s, g)
+        pool_tiles_before(TILES)

@@ -27,13 +27,13 @@ M_TILES = PHI_TILES + G_TILES
 WORDS = P
 WORD_BLOCKS = C // 2 // WORDS
 BANK_BLOCKS = 4
-FIRST_TILES = 4
-WEIGHTS_AHEAD = 2
+OPEN_TILES = 6
+assert M_TILES - OPEN_TILES == PASSES
 RUN = 4
 SHARED_BLOCKS = 2
-BLOCK_1_FROM = 5
-POOL_LAG = 2
-SUM_BANKS = 6
+POOL_LAG = 5
+BANKS = 8
+TURN_BANKS = 4
 TILES = M_TILES * N_BLOCKS
 
 FLOPS = 2 * M_TILES * P * C * PIXELS
@@ -59,8 +59,6 @@ def tile_attention_pa_kernel(tc, x, w_phi, w_g, out_0, out_1):
         keep = ctx.enter_context(tc.tile_pool(name="keep", bufs=1))
         w_stage = ctx.enter_context(tc.tile_pool(name="w_stage", bufs=3))
         x_stage = ctx.enter_context(tc.tile_pool(name="x_stage", bufs=3))
-        sums = ctx.enter_context(tc.psum_pool(name="sums", bufs=SUM_BANKS))
-        turned = ctx.enter_context(tc.psum_pool(name="turned", bufs=8 - SUM_BANKS))
         ctx.enter_context(tc.manual_schedule())
 
         identity = keep.tile([P, P], F32, name="identity")
@@ -111,7 +109,7 @@ def tile_attention_pa_kernel(tc, x, w_phi, w_g, out_0, out_1):
                     ].rearrange("(p e) n -> p e n", e=2),
                 )
 
-        def flip_weights(m):
+        def flip_weights(turned, m):
             grouped = w_stage.tile([P, C], BF16, name="w_grouped", tag="w_grouped", align_bytes=64)
             grouped_words = grouped[:].bitcast(F32).rearrange(
                 "p (g o u) -> p g o u", g=PASSES, o=P, u=2
@@ -155,7 +153,7 @@ def tile_attention_pa_kernel(tc, x, w_phi, w_g, out_0, out_1):
                 in_=x_grouped[(b, g)][:].rearrange("p n t -> p (n t)"),
             )
 
-        def open_sum(s):
+        def open_sum(sums, s):
             open_sums[s] = sums.tile([P, N_BLOCK], F32, name="acc", tag="acc")
 
         def multiply(s, g):
@@ -188,53 +186,49 @@ def tile_attention_pa_kernel(tc, x, w_phi, w_g, out_0, out_1):
                 )
                 pooled_tiles.append(s)
 
-        for m in range(FIRST_TILES):
+        for m in range(M_TILES):
             load_weights(m)
-        for g in range(PASSES):
-            load_x(0, g)
-        for m in range(FIRST_TILES, M_TILES):
-            load_weights(m)
-        for b in range(1, N_BLOCKS):
+        for b in range(N_BLOCKS):
             for g in range(PASSES):
                 load_x(b, g)
 
-        for m in range(FIRST_TILES):
-            flip_weights(m)
-            quantise_weights(m)
-            open_sum(m)
+        with tc.psum_pool(name="turned", bufs=TURN_BANKS) as turned:
+            for m in range(M_TILES):
+                flip_weights(turned, m)
+                quantise_weights(m)
 
-        regroup_x(0, 0)
-        for step in range(M_TILES):
-            if step + 1 < PASSES:
-                regroup_x(0, step + 1)
-            if FIRST_TILES <= step + WEIGHTS_AHEAD < M_TILES:
-                flip_weights(step + WEIGHTS_AHEAD)
-            if 0 <= step - BLOCK_1_FROM < PASSES:
-                regroup_x(1, step - BLOCK_1_FROM)
-            if step < PASSES:
-                quantise_x(0, step)
-            if FIRST_TILES <= step + WEIGHTS_AHEAD - 1 < M_TILES:
-                quantise_weights(step + WEIGHTS_AHEAD - 1)
-            if 0 <= step - BLOCK_1_FROM - 1 < PASSES:
-                quantise_x(1, step - BLOCK_1_FROM - 1)
-            if step < PASSES:
-                for m in range(FIRST_TILES):
-                    multiply(m, step)
-            else:
-                pool_tiles_before(step - POOL_LAG)
-                open_sum(step)
+        with tc.psum_pool(name="sums", bufs=BANKS, reuse_waits="tile") as sums:
+
+            def whole_tile(s):
+                pool_tiles_before(s - POOL_LAG)
+                open_sum(sums, s)
                 for g in range(PASSES):
-                    multiply(step, g)
+                    multiply(s, g)
 
-        for s in range(M_TILES, TILES):
-            b, m = divmod(s, M_TILES)
+            for s in range(OPEN_TILES):
+                open_sum(sums, s)
+            regroup_x(0, 0)
             for g in range(PASSES):
-                if b + 1 < N_BLOCKS and g * M_TILES // PASSES == m:
-                    regroup_x(b + 1, g)
-                if b + 1 < N_BLOCKS and g * M_TILES // PASSES + 2 == m:
-                    quantise_x(b + 1, g)
-            pool_tiles_before(s - POOL_LAG)
-            open_sum(s)
-            for g in range(PASSES):
-                multiply(s, g)
-        pool_tiles_before(TILES)
+                if g + 1 < PASSES:
+                    regroup_x(0, g + 1)
+                quantise_x(0, g)
+                for s in range(OPEN_TILES):
+                    multiply(s, g)
+
+            regroup_x(1, 0)
+            for s in range(OPEN_TILES, M_TILES):
+                g = s - OPEN_TILES
+                if g + 1 < PASSES:
+                    regroup_x(1, g + 1)
+                quantise_x(1, g)
+                whole_tile(s)
+
+            for s in range(M_TILES, TILES):
+                b, m = divmod(s, M_TILES)
+                for g in range(PASSES):
+                    if b + 1 < N_BLOCKS and g * M_TILES // PASSES == m:
+                        regroup_x(b + 1, g)
+                    if b + 1 < N_BLOCKS and g * M_TILES // PASSES + 2 == m:
+                        quantise_x(b + 1, g)
+                whole_tile(s)
+            pool_tiles_before(TILES)

@@ -140,7 +140,7 @@ def tile_attention_pa_kernel(tc, x, w_phi, w_g, out_0, out_1):
             )
             target = grouped[:].rearrange("p (c r) t -> p c t r", r=RUN)
             source = x_raw[b][g][:].rearrange("p t (c r) -> p c t r", r=RUN)
-            vector_runs = N_BLOCK // RUN // 2 if b < SHARED_BLOCKS else 0
+            vector_runs = (N_BLOCK // RUN) >> (b + 1) if b < SHARED_BLOCKS else 0
             if vector_runs > 0:
                 nc.vector.tensor_copy(out=target[:, :vector_runs], in_=source[:, :vector_runs])
             nc.scalar.copy(out=target[:, vector_runs:], in_=source[:, vector_runs:])

from contextlib import ExitStack

import concourse.mybir as mybir
from concourse.masks import make_identity

BF16 = mybir.dt.bfloat16
F32 = mybir.dt.float32
U32 = mybir.dt.uint32
U8 = mybir.dt.uint8
FP8X4 = mybir.dt.float8_e4m3fn_x4

P = 128
PACK = 4
K_PASS = P * PACK
C = 2048
PASSES = C // K_PASS
HEIGHT, WIDTH = 32, 64
PIXELS = HEIGHT * WIDTH
N_BLOCK = 512
N_BLOCKS = PIXELS // N_BLOCK
POOLED_ROWS = N_BLOCK // WIDTH // 2
POOLED_WIDTH = WIDTH // 2
POOLED_BLOCK = POOLED_ROWS * POOLED_WIDTH
PHI_TILES = 256 // P
G_TILES = 1024 // P
M_TILES = PHI_TILES + G_TILES
WORDS = P
WORD_BLOCKS = C // 2 // WORDS
BANK_BLOCKS = 4
OPEN_TILES = 6
assert M_TILES - OPEN_TILES == PASSES
RUN = 4
SHARED_BLOCKS = 2
POOL_LAG = 5
BANKS = 8
TURN_BANKS = 4
TILES = M_TILES * N_BLOCKS

FLOPS = 2 * M_TILES * P * C * PIXELS


def tile_attention_pa_kernel(tc, x, w_phi, w_g, out_0, out_1):
    nc = tc.nc
    x_rows = x.rearrange("b c h w -> (b c) (h w)")
    phi_rows = out_0.rearrange("b o m -> (b o) m")
    g_rows = out_1.rearrange("b o m -> (b o) m")

    def weight_rows(m):
        if m < PHI_TILES:
            return w_phi[m * P : (m + 1) * P, :]
        return w_g[(m - PHI_TILES) * P : (m - PHI_TILES + 1) * P, :]

    def output_rows(m):
        if m < PHI_TILES:
            return phi_rows[m * P : (m + 1) * P, :]
        return g_rows[(m - PHI_TILES) * P : (m - PHI_TILES + 1) * P, :]

    with ExitStack() as ctx:
        keep = ctx.enter_context(tc.tile_pool(name="keep", bufs=1))
        w_stage = ctx.enter_context(tc.tile_pool(name="w_stage", bufs=3))
        x_stage = ctx.enter_context(tc.tile_pool(name="x_stage", bufs=3))
        ctx.enter_context(tc.manual_schedule())

        identity = keep.tile([P, P], F32, name="identity")
        make_identity(nc, identity[:])

        w_raw = [keep.tile([P, C], BF16, name="w_raw%d" % m) for m in range(M_TILES)]
        w_codes = [
            keep.tile([P, PASSES * P], U32, name="w_codes%d" % m, align_bytes=64)
            for m in range(M_TILES)
        ]
        w_scales = [
            keep.tile([P, PASSES * P], U8, name="w_scales%d" % m, align_bytes=64)
            for m in range(M_TILES)
        ]
        x_raw = [
            [keep.tile([P, PACK, N_BLOCK], BF16, name="x_raw%d_%d" % (b, g)) for g in range(PASSES)]
            for b in range(N_BLOCKS)
        ]
        x_codes = [
            [
                keep.tile([P, N_BLOCK], U32, name="x_codes%d_%d" % (b, g), align_bytes=64)
                for g in range(PASSES)
            ]
            for b in range(N_BLOCKS)
        ]
        x_scales = [
            [
                keep.tile([P, N_BLOCK], U8, name="x_scales%d_%d" % (b, g), align_bytes=64)
                for g in range(PASSES)
            ]
            for b in range(N_BLOCKS)
        ]
        w_grouped = {}
        x_grouped = {}
        open_sums = {}
        pooled_tiles = []

        def load_weights(m):
            nc.sync.dma_start(out=w_raw[m][:], in_=weight_rows(m))

        def load_x(b, g):
            for u in range(2):
                first = g * K_PASS + u * 2 * P
                nc.sync.dma_start(
                    out=x_raw[b][g][:, 2 * u : 2 * u + 2, :],
                    in_=x_rows[
                        first : first + 2 * P, b * N_BLOCK : (b + 1) * N_BLOCK
                    ].rearrange("(p e) n -> p e n", e=2),
                )

        def flip_weights(turned, m):
            grouped = w_stage.tile([P, C], BF16, name="w_grouped", tag="w_grouped", align_bytes=64)
            grouped_words = grouped[:].bitcast(F32).rearrange(
                "p (g o u) -> p g o u", g=PASSES, o=P, u=2
            )
            raw_words = w_raw[m][:].bitcast(F32)
            passes_in_bank = BANK_BLOCKS // 2
            for bank in range(WORD_BLOCKS // BANK_BLOCKS):
                flipped = turned.tile([P, BANK_BLOCKS, P], F32, name="flipped", tag="flipped")
                for q in range(BANK_BLOCKS):
                    j = bank * BANK_BLOCKS + q
                    nc.tensor.transpose(
                        flipped[:, q, :], raw_words[:, j * WORDS : (j + 1) * WORDS], identity[:]
                    )
                nc.scalar.copy(
                    out=grouped_words[:, bank * passes_in_bank : (bank + 1) * passes_in_bank],
                    in_=flipped[:].rearrange("p (g u) o -> p g o u", u=2),
                )
            w_grouped[m] = grouped

        def quantise_weights(m):
            nc.vector.quantize_mx(
                out=w_codes[m][:].bitcast(FP8X4), scales=w_scales[m][:], in_=w_grouped[m][:]
            )

        def regroup_x(b, g):
            grouped = x_stage.tile(
                [P, N_BLOCK, PACK], BF16, name="x_grouped", tag="x_grouped", align_bytes=64
            )
            target = grouped[:].rearrange("p (c r) t -> p c t r", r=RUN)
            source = x_raw[b][g][:].rearrange("p t (c r) -> p c t r", r=RUN)
            vector_runs = (N_BLOCK // RUN) >> (b + 1) if b < SHARED_BLOCKS else 0
            if vector_runs > 0:
                nc.vector.tensor_copy(out=target[:, :vector_runs], in_=source[:, :vector_runs])
            nc.scalar.copy(out=target[:, vector_runs:], in_=source[:, vector_runs:])
            x_grouped[(b, g)] = grouped

        def quantise_x(b, g):
            nc.vector.quantize_mx(
                out=x_codes[b][g][:].bitcast(FP8X4),
                scales=x_scales[b][g][:],
                in_=x_grouped[(b, g)][:].rearrange("p n t -> p (n t)"),
            )

        def open_sum(sums, s):
            open_sums[s] = sums.tile([P, N_BLOCK], F32, name="acc", tag="acc")

        def multiply(s, g):
            b, m = divmod(s, M_TILES)
            nc.tensor.matmul_mx(
                out=open_sums[s][:],
                lhsT=w_codes[m][:, g * P : (g + 1) * P].bitcast(FP8X4),
                lhsT_scale=w_scales[m][:, g * P : (g + 1) * P],
                rhs=x_codes[b][g][:].bitcast(FP8X4),
                rhs_scale=x_scales[b][g][:],
                start=(g == 0),
                stop=(g == PASSES - 1),
            )

        def pool_tiles_before(limit):
            for s in range(len(pooled_tiles), limit):
                b, m = divmod(s, M_TILES)
                pooled = keep.tile([P, POOLED_ROWS, POOLED_WIDTH], F32, name="pooled%d" % s)
                nc.vector.tensor_reduce(
                    out=pooled[:],
                    in_=open_sums[s][:].rearrange(
                        "p (i a j b) -> p i j a b", i=POOLED_ROWS, a=2, j=POOLED_WIDTH, b=2
                    ),
                    axis=mybir.AxisListType.XY,
                    op=mybir.AluOpType.max,
                )
                nc.sync.dma_start(
                    out=output_rows(m)[:, b * POOLED_BLOCK : (b + 1) * POOLED_BLOCK],
                    in_=pooled[:].rearrange("p i j -> p (i j)"),
                )
                pooled_tiles.append(s)

        for m in range(M_TILES):
            load_weights(m)
        for b in range(N_BLOCKS):
            for g in range(PASSES):
                load_x(b, g)

        with tc.psum_pool(name="turned", bufs=TURN_BANKS) as turned:
            for m in range(M_TILES):
                flip_weights(turned, m)
                quantise_weights(m)

        with tc.psum_pool(name="sums", bufs=BANKS, reuse_waits="tile") as sums:

            def whole_tile(s):
                pool_tiles_before(s - POOL_LAG)
                open_sum(sums, s)
                for g in range(PASSES):
                    multiply(s, g)

            for s in range(OPEN_TILES):
                open_sum(sums, s)
            regroup_x(0, 0)
            for g in range(PASSES):
                if g + 1 < PASSES:
                    regroup_x(0, g + 1)
                quantise_x(0, g)
                for s in range(OPEN_TILES):
                    multiply(s, g)

            regroup_x(1, 0)
            for s in range(OPEN_TILES, M_TILES):
                g = s - OPEN_TILES
                if g + 1 < PASSES:
                    regroup_x(1, g + 1)
                quantise_x(1, g)
                whole_tile(s)

            for s in range(M_TILES, TILES):
                b, m = divmod(s, M_TILES)
                for g in range(PASSES):
                    if b + 1 < N_BLOCKS and g * M_TILES // PASSES == m:
                        regroup_x(b + 1, g)
                    if b + 1 < N_BLOCKS and g * M_TILES // PASSES + 2 == m:
                        quantise_x(b + 1, g)
                whole_tile(s)
            pool_tiles_before(TILES)
